import numpy as np
import ml_dtypes


def mxq(x, axis, fmt="e4m3"):
    dtype, down = {"e4m3": (ml_dtypes.float8_e4m3fn, 7), "e5m2": (ml_dtypes.float8_e5m2, 14)}[fmt]
    v = np.moveaxis(np.asarray(x, np.float32).astype(ml_dtypes.bfloat16).astype(np.float64), axis, -1)
    blocks = v.reshape(v.shape[:-1] + (-1, 32))
    amax = np.abs(blocks).max(-1, keepdims=True)
    byte = np.maximum(np.where(amax > 0, np.frexp(amax)[1] - 1 + 127, 0) - down, 1)
    scale = np.exp2(byte - 127.0)
    codes = (blocks / scale).astype(np.float32).astype(dtype).astype(np.float64)
    return np.moveaxis((codes * scale).reshape(v.shape), -1, axis)


WIDE = False


def mx_kscale(k):
    if not WIDE:
        return np.ones(k)
    levels = np.array([10, -10, 5, -5, 0])
    if k % 512:
        return np.exp2(np.random.permutation(np.resize(levels, k // 32))).repeat(32)
    a = np.empty((k // 512, 16))
    for p in range(k // 512):
        a[p, :8] = np.random.permutation(np.resize(levels, 8))
        for g in range(8):
            far = levels[np.abs(levels - a[p, g]) >= 10]
            a[p, g + 8] = far[np.random.randint(len(far))]
    return np.exp2(a.ravel()).repeat(32)


BF16 = ml_dtypes.bfloat16


def bf(x):
    return np.asarray(x, np.float32).astype(BF16)


def f64(x):
    return np.asarray(x).astype(np.float64)


B, CIN, P, COUT, W, H, HEADS = 2, 1024, 512, 2048, 16, 32, 4
N = W * H
EPS = 1e-5


def bn(y, g, b, m, v):
    return (y - f64(m)[None, :, None]) * (f64(g) / np.sqrt(f64(v) + EPS))[None, :, None] + f64(b)[None, :, None]


def setup_inputs():
    s, t = mx_kscale(P), mx_kscale(CIN)
    return {
        "h_attn": bf(np.maximum(np.random.standard_normal((B, P, N)), 0.0) * s[None, :, None]),
        "x": bf(np.random.standard_normal((B, CIN, N)) * t[None, :, None]),
        "conv3_w": bf(np.random.standard_normal((COUT, P)) * 1.5 / np.sqrt(P) / s[None, :]),
        "bn3_g": bf(np.random.uniform(0.5, 1.5, COUT)),
        "bn3_b": bf(np.random.standard_normal(COUT) * 0.3),
        "bn3_m": bf(np.random.standard_normal(COUT) * 0.3),
        "bn3_v": bf(np.random.uniform(0.5, 1.5, COUT)),
        "sc_w": bf(np.random.standard_normal((COUT, CIN)) / np.sqrt(CIN) / t[None, :]),
        "sc_b": bf(np.random.standard_normal(COUT) * 0.3),
        "scbn_g": bf(np.random.uniform(0.5, 1.5, COUT)),
        "scbn_b": bf(np.random.standard_normal(COUT) * 0.3),
        "scbn_m": bf(np.random.standard_normal(COUT) * 0.3),
        "scbn_v": bf(np.random.uniform(0.5, 1.5, COUT)),
    }


def reference(h_attn, x, conv3_w, bn3_g, bn3_b, bn3_m, bn3_v, sc_w, sc_b, scbn_g, scbn_b, scbn_m, scbn_v):
    main = bn(mxq(f64(conv3_w), 1, "e4m3") @ mxq(f64(h_attn), 1, "e4m3"), bn3_g, bn3_b, bn3_m, bn3_v)
    short = (mxq(f64(sc_w), 1, "e4m3") @ mxq(f64(x), 1, "e4m3")) + f64(sc_b)[None, :, None]
    short = bn(short, scbn_g, scbn_b, scbn_m, scbn_v)
    return np.maximum(main + short, 0.0)

@@ -1,0 +1,214 @@
+from contextlib import ExitStack
+
+import concourse.mybir as mybir
+from concourse.masks import make_identity
+
+F32 = mybir.dt.float32
+BF16 = mybir.dt.bfloat16
+U32 = mybir.dt.uint32
+U8 = mybir.dt.uint8
+FP8X4 = mybir.dt.float8_e4m3fn_x4
+ACT = mybir.ActivationFunctionType
+ALU = mybir.AluOpType
+
+P = 128
+PACK = 4
+K_PASS = P * PACK
+BATCH = 2
+POSITIONS = 512
+C_MAIN = 512
+C_SHORT = 1024
+C_ALL = C_MAIN + C_SHORT
+PASSES = C_ALL // K_PASS
+C_OUT = 2048
+SLOTS = C_OUT // P
+GROUP = 2
+GROUPS = SLOTS // GROUP
+UNITS_PER_BANK = 2
+BANKS_PER_GROUP = GROUP * PASSES // UNITS_PER_BANK
+EPS = 1e-5
+
+FLOPS = 2 * BATCH * C_OUT * C_ALL * POSITIONS
+
+
+def tile_bottleneck_transformer_pb_kernel(
+    tc, h_attn, x, conv3_w, bn3_g, bn3_b, bn3_m, bn3_v, sc_w, sc_b, scbn_g, scbn_b, scbn_m, scbn_v, out
+):
+    nc = tc.nc
+    with ExitStack() as ctx:
+        keep = ctx.enter_context(tc.tile_pool(name="keep", bufs=1))
+        act_stage = ctx.enter_context(tc.tile_pool(name="act_stage", bufs=3))
+        w_stage = ctx.enter_context(tc.tile_pool(name="w_stage", bufs=4))
+        bn_stage = ctx.enter_context(tc.tile_pool(name="bn_stage", bufs=4))
+        results = ctx.enter_context(tc.tile_pool(name="results", bufs=10))
+        banks = ctx.enter_context(tc.psum_pool(name="banks", bufs=8))
+        ctx.enter_context(tc.manual_schedule())
+
+        w_raw = keep.tile([P, SLOTS * C_ALL], BF16)
+        w_raw_slots = w_raw[:].rearrange("p (c k) -> p c k", c=SLOTS)
+        w_words = w_raw[:].bitcast(F32)
+        conv3_slots = conv3_w.rearrange("(p c) k -> p c k", c=SLOTS)
+        sc_slots = sc_w.rearrange("(p c) k -> p c k", c=SLOTS)
+        act_raw = [keep.tile([P, PASSES, PACK, POSITIONS], BF16, name="act_raw%d" % b) for b in range(BATCH)]
+        act_codes = [keep.tile([P, PASSES, POSITIONS], U32, name="act_codes%d" % b, align_bytes=64) for b in range(BATCH)]
+        act_scales = [keep.tile([P, PASSES, POSITIONS], U8, name="act_scales%d" % b, align_bytes=64) for b in range(BATCH)]
+        w_codes = keep.tile([P, SLOTS * PASSES * P], U32, align_bytes=64)
+        w_scales = keep.tile([P, SLOTS * PASSES * P], U8, align_bytes=64)
+        out_slots = [out[b].rearrange("(p c) n -> p c n", c=SLOTS) for b in range(BATCH)]
+
+        def load_weights(g):
+            slots = slice(g * GROUP, (g + 1) * GROUP)
+            nc.sync.dma_start(out=w_raw_slots[:, slots, 0:C_MAIN], in_=conv3_slots[:, slots, :])
+            nc.sync.dma_start(out=w_raw_slots[:, slots, C_MAIN:C_ALL], in_=sc_slots[:, slots, :])
+
+        def load_activations(b):
+            for k_pass in range(PASSES):
+                rows = h_attn[b] if k_pass == 0 else x[b, (k_pass - 1) * K_PASS : k_pass * K_PASS, :]
+                nc.sync.dma_start(out=act_raw[b][:, k_pass], in_=rows.rearrange("(p t) n -> p t n", t=PACK))
+
+        load_activations(0)
+        for g in range(GROUPS // 2):
+            load_weights(g)
+        load_activations(1)
+        for g in range(GROUPS // 2, GROUPS):
+            load_weights(g)
+
+        vectors = keep.tile([P, 9, SLOTS], BF16)
+        V_VAR, V_GAIN, V_MEAN, V_SHIFT, V_BIAS = 0, 2, 4, 6, 8
+        for i, vec in enumerate((bn3_v, scbn_v, bn3_g, scbn_g, bn3_m, scbn_m, bn3_b, scbn_b, sc_b)):
+            nc.scalar.dma_start(out=vectors[:, i, :], in_=vec.rearrange("(p c) -> p c", c=SLOTS))
+
+        identity = keep.tile([P, P], F32)
+        make_identity(nc, identity[:])
+
+        act_grouped = {}
+
+        def regroup_activations(b, k_pass):
+            grouped = act_stage.tile([P, POSITIONS, PACK], BF16, name="act_grouped", align_bytes=64)
+            nc.vector.tensor_copy(
+                out=grouped[:].rearrange("p (c i) t -> p c t i", i=4),
+                in_=act_raw[b][:, k_pass].rearrange("p t (c i) -> p c t i", i=4),
+            )
+            act_grouped[(b, k_pass)] = grouped
+
+        def quantise_activations(b, k_pass):
+            nc.vector.quantize_mx(
+                out=act_codes[b][:, k_pass, :].bitcast(FP8X4),
+                scales=act_scales[b][:, k_pass, :],
+                in_=act_grouped[(b, k_pass)][:].rearrange("p n t -> p (n t)"),
+            )
+
+        turned = {}
+
+        def transpose_weights(g):
+            for j in range(g * BANKS_PER_GROUP, (g + 1) * BANKS_PER_GROUP):
+                turned[j] = banks.tile([P, UNITS_PER_BANK, 2, P], F32, name="turned", tag="bank")
+                for a in range(UNITS_PER_BANK):
+                    for u in range(2):
+                        first = (j * UNITS_PER_BANK + a) * 2 * P
+                        nc.tensor.transpose(turned[j][:, a, u, :], w_words[:, first + u : first + 2 * P : 2], identity[:])
+
+        w_grouped = {}
+
+        def copy_out_weights(g):
+            for j in range(g * BANKS_PER_GROUP, (g + 1) * BANKS_PER_GROUP):
+                w_grouped[j] = w_stage.tile([P, UNITS_PER_BANK * P * PACK], BF16, name="w_grouped", align_bytes=64)
+                nc.scalar.copy(
+                    out=w_grouped[j][:].bitcast(F32).rearrange("p (a m u) -> p a m u", a=UNITS_PER_BANK, u=2),
+                    in_=turned[j][:].rearrange("p a u m -> p a m u"),
+                )
+
+        def quantise_weights(g):
+            for j in range(g * BANKS_PER_GROUP, (g + 1) * BANKS_PER_GROUP):
+                cols = slice(j * UNITS_PER_BANK * P, (j + 1) * UNITS_PER_BANK * P)
+                nc.vector.quantize_mx(out=w_codes[:, cols].bitcast(FP8X4), scales=w_scales[:, cols], in_=w_grouped[j][:])
+
+        def multiply(acc, b, c, passes):
+            for k_pass in passes:
+                cols = slice((c * PASSES + k_pass) * P, (c * PASSES + k_pass + 1) * P)
+                nc.tensor.matmul_mx(
+                    out=acc[:],
+                    lhsT=w_codes[:, cols].bitcast(FP8X4),
+                    lhsT_scale=w_scales[:, cols],
+                    rhs=act_codes[b][:, k_pass, :].bitcast(FP8X4),
+                    rhs_scale=act_scales[b][:, k_pass, :],
+                    start=(k_pass == passes[0]),
+                    stop=(k_pass == passes[-1]),
+                )
+
+        def multiply_group(b, g):
+            products = []
+            for c in range(g * GROUP, (g + 1) * GROUP):
+                main = banks.tile([P, POSITIONS], F32, name="main", tag="bank")
+                multiply(main, b, c, (0,))
+                short = banks.tile([P, POSITIONS], F32, name="short", tag="bank")
+                multiply(short, b, c, (1, 2))
+                products.append((c, main, short))
+            return products
+
+        def batch_norms_and_sum(products):
+            result = results.tile([P, GROUP, POSITIONS], F32, name="result")
+            main_bn = []
+            for c, main, short in products:
+                main_bn.append(bn_stage.tile([P, POSITIONS], F32, name="main_bn"))
+                nc.scalar.activation(
+                    out=main_bn[-1][:], in_=main[:], func=ACT.Identity, scale=gain[:, 0, c : c + 1], bias=shift[:, c : c + 1]
+                )
+            for i, (c, main, short) in enumerate(products):
+                nc.vector.scalar_tensor_tensor(
+                    out=result[:, i, :], in0=short[:], scalar=gain[:, 1, c : c + 1], in1=main_bn[i][:], op0=ALU.mult, op1=ALU.add
+                )
+            return result
+
+        def relu_and_store(b, g, result):
+            if g % 4 == 1:
+                nc.scalar.activation(out=result[:], in_=result[:], func=ACT.Relu)
+            else:
+                nc.vector.tensor_scalar_max(out=result[:], in0=result[:], scalar1=0.0)
+            nc.sync.dma_start(out=out_slots[b][:, g * GROUP : (g + 1) * GROUP, :], in_=result[:])
+
+        spread = keep.tile([P, 2, SLOTS], F32)
+        gain = keep.tile([P, 2, SLOTS], F32)
+        centre = keep.tile([P, 2, SLOTS], F32)
+        shift = keep.tile([P, SLOTS], F32)
+        nc.vector.tensor_scalar_add(out=spread[:], in0=vectors[:, V_VAR : V_VAR + 2, :], scalar1=EPS)
+        nc.scalar.sqrt(out=spread[:], in_=spread[:])
+        regroup_activations(0, 0)
+        regroup_activations(0, 1)
+        quantise_activations(0, 0)
+        regroup_activations(0, 2)
+        quantise_activations(0, 1)
+        nc.vector.reciprocal(out=gain[:], in_=spread[:])
+        nc.vector.tensor_mul(out=gain[:], in0=gain[:], in1=vectors[:, V_GAIN : V_GAIN + 2, :])
+        nc.vector.tensor_copy(out=centre[:, 0, :], in_=vectors[:, V_MEAN, :])
+        nc.vector.tensor_sub(out=centre[:, 1, :], in0=vectors[:, V_MEAN + 1, :], in1=vectors[:, V_BIAS, :])
+        nc.vector.tensor_mul(out=centre[:], in0=centre[:], in1=gain[:])
+        nc.vector.tensor_add(out=shift[:], in0=vectors[:, V_SHIFT, :], in1=vectors[:, V_SHIFT + 1, :])
+        nc.vector.tensor_sub(out=shift[:], in0=shift[:], in1=centre[:, 0, :])
+        nc.vector.tensor_sub(out=shift[:], in0=shift[:], in1=centre[:, 1, :])
+        quantise_activations(0, 2)
+        transpose_weights(0)
+        copy_out_weights(0)
+        transpose_weights(1)
+        quantise_weights(0)
+
+        waiting = []
+        for g in range(GROUPS):
+            if g + 1 < GROUPS:
+                copy_out_weights(g + 1)
+                quantise_weights(g + 1)
+            products = multiply_group(0, g)
+            if g + 2 < GROUPS:
+                transpose_weights(g + 2)
+            waiting.append((0, g, batch_norms_and_sum(products)))
+            if len(waiting) > 1:
+                relu_and_store(*waiting.pop(0))
+            if 1 <= g <= PASSES:
+                regroup_activations(1, g - 1)
+            if 2 <= g <= PASSES + 1:
+                quantise_activations(1, g - 2)
+
+        for g in range(GROUPS):
+            waiting.append((1, g, batch_norms_and_sum(multiply_group(1, g))))
+            relu_and_store(*waiting.pop(0))
+        relu_and_store(*waiting.pop(0))

@@ -24,8 +24,7 @@ C_OUT = 2048
 SLOTS = C_OUT // P
 GROUP = 2
 GROUPS = SLOTS // GROUP
-UNITS_PER_BANK = 2
-BANKS_PER_GROUP = GROUP * PASSES // UNITS_PER_BANK
+UNIT = P
 EPS = 1e-5
 
 FLOPS = 2 * BATCH * C_OUT * C_ALL * POSITIONS
@@ -44,52 +43,75 @@ def tile_bottleneck_transformer_pb_kernel(
         banks = ctx.enter_context(tc.psum_pool(name="banks", bufs=8))
         ctx.enter_context(tc.manual_schedule())
 
-        w_raw = keep.tile([P, SLOTS * C_ALL], BF16)
-        w_raw_slots = w_raw[:].rearrange("p (c k) -> p c k", c=SLOTS)
-        w_words = w_raw[:].bitcast(F32)
+        main_raw = [keep.tile([P, GROUP, C_MAIN], BF16, name="main_raw%d" % g) for g in range(GROUPS)]
+        short_raw = [keep.tile([P, GROUP, C_SHORT], BF16, name="short_raw%d" % g) for g in range(GROUPS)]
         conv3_slots = conv3_w.rearrange("(p c) k -> p c k", c=SLOTS)
         sc_slots = sc_w.rearrange("(p c) k -> p c k", c=SLOTS)
         act_raw = [keep.tile([P, PASSES, PACK, POSITIONS], BF16, name="act_raw%d" % b) for b in range(BATCH)]
         act_codes = [keep.tile([P, PASSES, POSITIONS], U32, name="act_codes%d" % b, align_bytes=64) for b in range(BATCH)]
         act_scales = [keep.tile([P, PASSES, POSITIONS], U8, name="act_scales%d" % b, align_bytes=64) for b in range(BATCH)]
-        w_codes = keep.tile([P, SLOTS * PASSES * P], U32, align_bytes=64)
-        w_scales = keep.tile([P, SLOTS * PASSES * P], U8, align_bytes=64)
+        w_codes = keep.tile([P, GROUPS, PASSES, GROUP * UNIT], U32, align_bytes=64)
+        w_scales = keep.tile([P, GROUPS, PASSES, GROUP * UNIT], U8, align_bytes=64)
         out_slots = [out[b].rearrange("(p c) n -> p c n", c=SLOTS) for b in range(BATCH)]
 
+        def group_slots(g):
+            return slice(g * GROUP, (g + 1) * GROUP)
+
+        def load_main_weights(g):
+            nc.sync.dma_start(out=main_raw[g][:], in_=conv3_slots[:, group_slots(g), :])
+
+        def load_short_weights(g):
+            nc.sync.dma_start(out=short_raw[g][:], in_=sc_slots[:, group_slots(g), :])
+
         def load_weights(g):
-            slots = slice(g * GROUP, (g + 1) * GROUP)
-            nc.sync.dma_start(out=w_raw_slots[:, slots, 0:C_MAIN], in_=conv3_slots[:, slots, :])
-            nc.sync.dma_start(out=w_raw_slots[:, slots, C_MAIN:C_ALL], in_=sc_slots[:, slots, :])
+            load_main_weights(g)
+            load_short_weights(g)
 
-        def load_activations(b):
-            for k_pass in range(PASSES):
-                rows = h_attn[b] if k_pass == 0 else x[b, (k_pass - 1) * K_PASS : k_pass * K_PASS, :]
-                nc.sync.dma_start(out=act_raw[b][:, k_pass], in_=rows.rearrange("(p t) n -> p t n", t=PACK))
+        def load_activations(b, k_pass):
+            rows = h_attn[b] if k_pass == 0 else x[b, (k_pass - 1) * K_PASS : k_pass * K_PASS, :]
+            nc.sync.dma_start(out=act_raw[b][:, k_pass], in_=rows.rearrange("(p t) n -> p t n", t=PACK))
 
-        load_activations(0)
-        for g in range(GROUPS // 2):
-            load_weights(g)
-        load_activations(1)
-        for g in range(GROUPS // 2, GROUPS):
-            load_weights(g)
-
-        vectors = keep.tile([P, 9, SLOTS], BF16)
-        V_VAR, V_GAIN, V_MEAN, V_SHIFT, V_BIAS = 0, 2, 4, 6, 8
-        for i, vec in enumerate((bn3_v, scbn_v, bn3_g, scbn_g, bn3_m, scbn_m, bn3_b, scbn_b, sc_b)):
-            nc.scalar.dma_start(out=vectors[:, i, :], in_=vec.rearrange("(p c) -> p c", c=SLOTS))
+        dummy = keep.tile([P, 2], F32)
+        nc.vector.memset(dummy[:, 0:1], 1.0)
+        nc.scalar.sqrt(out=dummy[:, 1:2], in_=dummy[:, 0:1])
 
         identity = keep.tile([P, P], F32)
         make_identity(nc, identity[:])
 
+        vectors = keep.tile([P, 9, SLOTS], BF16)
+        V_VAR, V_GAIN, V_MEAN, V_SHIFT, V_BIAS = 0, 2, 4, 6, 8
+        for i, vec in enumerate((bn3_v, scbn_v, bn3_g, scbn_g, bn3_m, scbn_m, bn3_b, scbn_b, sc_b)):
+            queue = nc.scalar if i < V_SHIFT else nc.gpsimd
+            queue.dma_start(out=vectors[:, i, :], in_=vec.rearrange("(p c) -> p c", c=SLOTS))
+
+        load_activations(0, 0)
+        load_main_weights(0)
+        load_activations(0, 1)
+        load_activations(0, 2)
+        load_short_weights(0)
+        for g in range(1, GROUPS // 2):
+            load_weights(g)
+        for k_pass in range(PASSES):
+            load_activations(1, k_pass)
+        for g in range(GROUPS // 2, GROUPS):
+            load_weights(g)
+
         act_grouped = {}
 
-        def regroup_activations(b, k_pass):
-            grouped = act_stage.tile([P, POSITIONS, PACK], BF16, name="act_grouped", align_bytes=64)
-            nc.vector.tensor_copy(
-                out=grouped[:].rearrange("p (c i) t -> p c t i", i=4),
-                in_=act_raw[b][:, k_pass].rearrange("p t (c i) -> p c t i", i=4),
-            )
-            act_grouped[(b, k_pass)] = grouped
+        def regroup_activations(b, k_pass, shares):
+            grouped = act_grouped.get((b, k_pass))
+            if grouped is None:
+                grouped = act_stage.tile([P, POSITIONS, PACK], BF16, name="act_grouped", align_bytes=64)
+                act_grouped[(b, k_pass)] = grouped
+            for copy, first, end in shares:
+                copy(
+                    out=grouped[:, first:end, :].rearrange("p (c i) t -> p c t i", i=4),
+                    in_=act_raw[b][:, k_pass, :, first:end].rearrange("p t (c i) -> p c t i", i=4),
+                )
+
+        WHOLE = ((nc.vector.tensor_copy, 0, POSITIONS),)
+        SHARED = ((nc.vector.tensor_copy, 0, 352), (nc.scalar.copy, 352, POSITIONS))
+        HALVES = (((nc.vector.tensor_copy, 0, 256),), ((nc.vector.tensor_copy, 256, POSITIONS),))
 
         def quantise_activations(b, k_pass):
             nc.vector.quantize_mx(
@@ -100,72 +122,69 @@ def tile_bottleneck_transformer_pb_kernel(
 
         turned = {}
 
-        def transpose_weights(g):
-            for j in range(g * BANKS_PER_GROUP, (g + 1) * BANKS_PER_GROUP):
-                turned[j] = banks.tile([P, UNITS_PER_BANK, 2, P], F32, name="turned", tag="bank")
-                for a in range(UNITS_PER_BANK):
-                    for u in range(2):
-                        first = (j * UNITS_PER_BANK + a) * 2 * P
-                        nc.tensor.transpose(turned[j][:, a, u, :], w_words[:, first + u : first + 2 * P : 2], identity[:])
+        def transpose_weights(g, k_pass):
+            bank = banks.tile([P, GROUP, 2, P], F32, name="turned", tag="bank")
+            turned[(g, k_pass)] = bank
+            raw, first = (main_raw[g], 0) if k_pass == 0 else (short_raw[g], (k_pass - 1) * K_PASS)
+            for i in range(GROUP):
+                words = raw[:, i, first : first + K_PASS].bitcast(F32)
+                for u in range(2):
+                    nc.tensor.transpose(bank[:, i, u, :], words[:, u : 2 * P : 2], identity[:])
 
         w_grouped = {}
 
-        def copy_out_weights(g):
-            for j in range(g * BANKS_PER_GROUP, (g + 1) * BANKS_PER_GROUP):
-                w_grouped[j] = w_stage.tile([P, UNITS_PER_BANK * P * PACK], BF16, name="w_grouped", align_bytes=64)
-                nc.scalar.copy(
-                    out=w_grouped[j][:].bitcast(F32).rearrange("p (a m u) -> p a m u", a=UNITS_PER_BANK, u=2),
-                    in_=turned[j][:].rearrange("p a u m -> p a m u"),
-                )
+        def copy_out_weights(g, k_pass):
+            grouped = w_stage.tile([P, GROUP * UNIT * PACK], BF16, name="w_grouped", align_bytes=64)
+            w_grouped[(g, k_pass)] = grouped
+            nc.scalar.copy(
+                out=grouped[:].bitcast(F32).rearrange("p (i m u) -> p i m u", i=GROUP, u=2),
+                in_=turned[(g, k_pass)][:].rearrange("p i u m -> p i m u"),
+            )
 
-        def quantise_weights(g):
-            for j in range(g * BANKS_PER_GROUP, (g + 1) * BANKS_PER_GROUP):
-                cols = slice(j * UNITS_PER_BANK * P, (j + 1) * UNITS_PER_BANK * P)
-                nc.vector.quantize_mx(out=w_codes[:, cols].bitcast(FP8X4), scales=w_scales[:, cols], in_=w_grouped[j][:])
+        def quantise_weights(g, k_pass):
+            nc.vector.quantize_mx(
+                out=w_codes[:, g, k_pass, :].bitcast(FP8X4), scales=w_scales[:, g, k_pass, :], in_=w_grouped[(g, k_pass)][:]
+            )
 
-        def multiply(acc, b, c, passes):
+        def multiply(b, c, passes, name):
+            acc = banks.tile([P, POSITIONS], F32, name=name, tag="bank")
+            g, i = divmod(c, GROUP)
             for k_pass in passes:
-                cols = slice((c * PASSES + k_pass) * P, (c * PASSES + k_pass + 1) * P)
                 nc.tensor.matmul_mx(
                     out=acc[:],
-                    lhsT=w_codes[:, cols].bitcast(FP8X4),
-                    lhsT_scale=w_scales[:, cols],
+                    lhsT=w_codes[:, g, k_pass, i * UNIT : (i + 1) * UNIT].bitcast(FP8X4),
+                    lhsT_scale=w_scales[:, g, k_pass, i * UNIT : (i + 1) * UNIT],
                     rhs=act_codes[b][:, k_pass, :].bitcast(FP8X4),
                     rhs_scale=act_scales[b][:, k_pass, :],
                     start=(k_pass == passes[0]),
                     stop=(k_pass == passes[-1]),
                 )
+            return acc
 
-        def multiply_group(b, g):
-            products = []
-            for c in range(g * GROUP, (g + 1) * GROUP):
-                main = banks.tile([P, POSITIONS], F32, name="main", tag="bank")
-                multiply(main, b, c, (0,))
-                short = banks.tile([P, POSITIONS], F32, name="short", tag="bank")
-                multiply(short, b, c, (1, 2))
-                products.append((c, main, short))
-            return products
+        def multiply_main(b, c):
+            return multiply(b, c, (0,), "main")
 
-        def batch_norms_and_sum(products):
-            result = results.tile([P, GROUP, POSITIONS], F32, name="result")
-            main_bn = []
-            for c, main, short in products:
-                main_bn.append(bn_stage.tile([P, POSITIONS], F32, name="main_bn"))
-                nc.scalar.activation(
-                    out=main_bn[-1][:], in_=main[:], func=ACT.Identity, scale=gain[:, 0, c : c + 1], bias=shift[:, c : c + 1]
-                )
-            for i, (c, main, short) in enumerate(products):
-                nc.vector.scalar_tensor_tensor(
-                    out=result[:, i, :], in0=short[:], scalar=gain[:, 1, c : c + 1], in1=main_bn[i][:], op0=ALU.mult, op1=ALU.add
-                )
-            return result
+        def multiply_short(b, c):
+            return multiply(b, c, (1, 2), "short")
 
-        def relu_and_store(b, g, result):
-            if g % 4 == 1:
-                nc.scalar.activation(out=result[:], in_=result[:], func=ACT.Relu)
+        def norm_main(c, main):
+            main_bn = bn_stage.tile([P, POSITIONS], F32, name="main_bn")
+            nc.scalar.activation(
+                out=main_bn[:], in_=main[:], func=ACT.Identity, scale=gain[:, 0, c : c + 1], bias=shift[:, c : c + 1]
+            )
+            return main_bn
+
+        def add_short(c, short, main_bn, total):
+            nc.vector.scalar_tensor_tensor(
+                out=total, in0=short[:], scalar=gain[:, 1, c : c + 1], in1=main_bn[:], op0=ALU.mult, op1=ALU.add
+            )
+
+        def relu_and_store(b, slots, result, on_scalar):
+            if on_scalar:
+                nc.scalar.activation(out=result, in_=result, func=ACT.Relu)
             else:
-                nc.vector.tensor_scalar_max(out=result[:], in0=result[:], scalar1=0.0)
-            nc.sync.dma_start(out=out_slots[b][:, g * GROUP : (g + 1) * GROUP, :], in_=result[:])
+                nc.vector.tensor_scalar_max(out=result, in0=result, scalar1=0.0)
+            nc.sync.dma_start(out=out_slots[b][:, slots, :], in_=result)
 
         spread = keep.tile([P, 2, SLOTS], F32)
         gain = keep.tile([P, 2, SLOTS], F32)
@@ -173,42 +192,76 @@ def tile_bottleneck_transformer_pb_kernel(
         shift = keep.tile([P, SLOTS], F32)
         nc.vector.tensor_scalar_add(out=spread[:], in0=vectors[:, V_VAR : V_VAR + 2, :], scalar1=EPS)
         nc.scalar.sqrt(out=spread[:], in_=spread[:])
-        regroup_activations(0, 0)
-        regroup_activations(0, 1)
-        quantise_activations(0, 0)
-        regroup_activations(0, 2)
-        quantise_activations(0, 1)
+        transpose_weights(0, 0)
+        regroup_activations(0, 0, WHOLE)
         nc.vector.reciprocal(out=gain[:], in_=spread[:])
+        copy_out_weights(0, 0)
+        quantise_activations(0, 0)
         nc.vector.tensor_mul(out=gain[:], in0=gain[:], in1=vectors[:, V_GAIN : V_GAIN + 2, :])
-        nc.vector.tensor_copy(out=centre[:, 0, :], in_=vectors[:, V_MEAN, :])
+        quantise_weights(0, 0)
+        mains = [multiply_main(0, c) for c in range(GROUP)]
+        nc.vector.tensor_mul(out=centre[:, 0, :], in0=gain[:, 0, :], in1=vectors[:, V_MEAN, :])
         nc.vector.tensor_sub(out=centre[:, 1, :], in0=vectors[:, V_MEAN + 1, :], in1=vectors[:, V_BIAS, :])
-        nc.vector.tensor_mul(out=centre[:], in0=centre[:], in1=gain[:])
+        regroup_activations(0, 1, SHARED)
+        nc.vector.tensor_mul(out=centre[:, 1, :], in0=centre[:, 1, :], in1=gain[:, 1, :])
         nc.vector.tensor_add(out=shift[:], in0=vectors[:, V_SHIFT, :], in1=vectors[:, V_SHIFT + 1, :])
+        regroup_activations(0, 2, SHARED)
         nc.vector.tensor_sub(out=shift[:], in0=shift[:], in1=centre[:, 0, :])
+        quantise_activations(0, 1)
         nc.vector.tensor_sub(out=shift[:], in0=shift[:], in1=centre[:, 1, :])
+        for k_pass in (1, 2):
+            transpose_weights(0, k_pass)
+            copy_out_weights(0, k_pass)
         quantise_activations(0, 2)
-        transpose_weights(0)
-        copy_out_weights(0)
-        transpose_weights(1)
-        quantise_weights(0)
+        quantise_weights(0, 1)
+        quantise_weights(0, 2)
+        for k_pass in range(PASSES):
+            transpose_weights(1, k_pass)
 
         waiting = []
         for g in range(GROUPS):
-            if g + 1 < GROUPS:
-                copy_out_weights(g + 1)
-                quantise_weights(g + 1)
-            products = multiply_group(0, g)
+            c0, c1 = g * GROUP, g * GROUP + 1
+            ahead = g + 1 < GROUPS
+            if ahead:
+                copy_out_weights(g + 1, 0)
+                quantise_weights(g + 1, 0)
+            if g > 0:
+                mains = [multiply_main(0, c) for c in (c0, c1)]
+            main_bn0 = norm_main(c0, mains[0])
+            if ahead:
+                copy_out_weights(g + 1, 1)
+                quantise_weights(g + 1, 1)
+            main_bn1 = norm_main(c1, mains[1])
+            if ahead:
+                copy_out_weights(g + 1, 2)
+            shorts = [multiply_short(0, c) for c in (c0, c1)]
+            result = results.tile([P, GROUP, POSITIONS], F32, name="result")
+            add_short(c0, shorts[0], main_bn0, result[:, 0, :])
+            if ahead:
+                quantise_weights(g + 1, 2)
+            add_short(c1, shorts[1], main_bn1, result[:, 1, :])
             if g + 2 < GROUPS:
-                transpose_weights(g + 2)
-            waiting.append((0, g, batch_norms_and_sum(products)))
+                for k_pass in range(PASSES):
+                    transpose_weights(g + 2, k_pass)
+            waiting.append((0, group_slots(g), result[:], g % 2 == 0))
             if len(waiting) > 1:
                 relu_and_store(*waiting.pop(0))
-            if 1 <= g <= PASSES:
-                regroup_activations(1, g - 1)
-            if 2 <= g <= PASSES + 1:
-                quantise_activations(1, g - 2)
+            if g >= 2 and g % 2 == 0:
+                quantise_activations(1, (g - 2) // 2)
+            if g < 2 * PASSES:
+                regroup_activations(1, g // 2, HALVES[g % 2])
 
         for g in range(GROUPS):
-            waiting.append((1, g, batch_norms_and_sum(multiply_group(1, g))))
+            c0, c1 = g * GROUP, g * GROUP + 1
+            mains = [multiply_main(1, c) for c in (c0, c1)]
+            main_bn0 = norm_main(c0, mains[0])
+            main_bn1 = norm_main(c1, mains[1])
+            shorts = [multiply_short(1, c) for c in (c0, c1)]
+            result = results.tile([P, GROUP, POSITIONS], F32, name="result")
+            add_short(c0, shorts[0], main_bn0, result[:, 0, :])
+            add_short(c1, shorts[1], main_bn1, result[:, 1, :])
             relu_and_store(*waiting.pop(0))
-        relu_and_store(*waiting.pop(0))
+            if g + 1 < GROUPS:
+                waiting.append((1, group_slots(g), result[:], g % 2 == 0))
+        relu_and_store(1, slice(c0, c0 + 1), result[:, 0:1, :], True)
+        relu_and_store(1, slice(c1, c1 + 1), result[:, 1:2, :], False)

@@ -26,6 +26,8 @@ GROUP = 2
 GROUPS = SLOTS // GROUP
 UNIT = P
 EPS = 1e-5
+STEPS = BATCH * GROUPS
+LEAD = 3
 
 FLOPS = 2 * BATCH * C_OUT * C_ALL * POSITIONS
 
@@ -37,8 +39,8 @@ def tile_bottleneck_transformer_pb_kernel(
     with ExitStack() as ctx:
         keep = ctx.enter_context(tc.tile_pool(name="keep", bufs=1))
         act_stage = ctx.enter_context(tc.tile_pool(name="act_stage", bufs=3))
-        w_stage = ctx.enter_context(tc.tile_pool(name="w_stage", bufs=4))
-        bn_stage = ctx.enter_context(tc.tile_pool(name="bn_stage", bufs=4))
+        w_stage = ctx.enter_context(tc.tile_pool(name="w_stage", bufs=3))
+        bn_stage = ctx.enter_context(tc.tile_pool(name="bn_stage", bufs=2 * (LEAD + 2)))
         results = ctx.enter_context(tc.tile_pool(name="results", bufs=10))
         banks = ctx.enter_context(tc.psum_pool(name="banks", bufs=8))
         ctx.enter_context(tc.manual_schedule())
@@ -81,20 +83,31 @@ def tile_bottleneck_transformer_pb_kernel(
         vectors = keep.tile([P, 9, SLOTS], BF16)
         V_VAR, V_GAIN, V_MEAN, V_SHIFT, V_BIAS = 0, 2, 4, 6, 8
         for i, vec in enumerate((bn3_v, scbn_v, bn3_g, scbn_g, bn3_m, scbn_m, bn3_b, scbn_b, sc_b)):
-            queue = nc.scalar if i < V_SHIFT else nc.gpsimd
+            queue = nc.scalar if i < V_MEAN else nc.gpsimd
             queue.dma_start(out=vectors[:, i, :], in_=vec.rearrange("(p c) -> p c", c=SLOTS))
 
         load_activations(0, 0)
         load_main_weights(0)
+        load_main_weights(1)
+        load_main_weights(2)
         load_activations(0, 1)
-        load_activations(0, 2)
         load_short_weights(0)
-        for g in range(1, GROUPS // 2):
-            load_weights(g)
-        for k_pass in range(PASSES):
-            load_activations(1, k_pass)
-        for g in range(GROUPS // 2, GROUPS):
-            load_weights(g)
+        load_activations(0, 2)
+        load_main_weights(3)
+        load_short_weights(1)
+        load_main_weights(4)
+        load_short_weights(2)
+        load_main_weights(5)
+        load_activations(1, 0)
+        load_short_weights(3)
+        load_main_weights(6)
+        load_activations(1, 1)
+        load_short_weights(4)
+        load_main_weights(7)
+        load_short_weights(5)
+        load_activations(1, 2)
+        load_short_weights(6)
+        load_short_weights(7)
 
         act_grouped = {}
 
@@ -122,69 +135,84 @@ def tile_bottleneck_transformer_pb_kernel(
 
         turned = {}
 
-        def transpose_weights(g, k_pass):
-            bank = banks.tile([P, GROUP, 2, P], F32, name="turned", tag="bank")
-            turned[(g, k_pass)] = bank
-            raw, first = (main_raw[g], 0) if k_pass == 0 else (short_raw[g], (k_pass - 1) * K_PASS)
-            for i in range(GROUP):
-                words = raw[:, i, first : first + K_PASS].bitcast(F32)
-                for u in range(2):
-                    nc.tensor.transpose(bank[:, i, u, :], words[:, u : 2 * P : 2], identity[:])
+        def transpose_weights(g, passes):
+            for k_pass in passes:
+                bank = banks.tile([P, GROUP, 2, P], F32, name="turned", tag="bank")
+                turned[(g, k_pass)] = bank
+                raw, first = (main_raw[g], 0) if k_pass == 0 else (short_raw[g], (k_pass - 1) * K_PASS)
+                for i in range(GROUP):
+                    words = raw[:, i, first : first + K_PASS].bitcast(F32)
+                    for u in range(2):
+                        nc.tensor.transpose(bank[:, i, u, :], words[:, u : 2 * P : 2], identity[:])
 
         w_grouped = {}
 
-        def copy_out_weights(g, k_pass):
-            grouped = w_stage.tile([P, GROUP * UNIT * PACK], BF16, name="w_grouped", align_bytes=64)
-            w_grouped[(g, k_pass)] = grouped
-            nc.scalar.copy(
-                out=grouped[:].bitcast(F32).rearrange("p (i m u) -> p i m u", i=GROUP, u=2),
-                in_=turned[(g, k_pass)][:].rearrange("p i u m -> p i m u"),
-            )
-
-        def quantise_weights(g, k_pass):
-            nc.vector.quantize_mx(
-                out=w_codes[:, g, k_pass, :].bitcast(FP8X4), scales=w_scales[:, g, k_pass, :], in_=w_grouped[(g, k_pass)][:]
-            )
-
-        def multiply(b, c, passes, name):
-            acc = banks.tile([P, POSITIONS], F32, name=name, tag="bank")
-            g, i = divmod(c, GROUP)
-            for k_pass in passes:
-                nc.tensor.matmul_mx(
-                    out=acc[:],
-                    lhsT=w_codes[:, g, k_pass, i * UNIT : (i + 1) * UNIT].bitcast(FP8X4),
-                    lhsT_scale=w_scales[:, g, k_pass, i * UNIT : (i + 1) * UNIT],
-                    rhs=act_codes[b][:, k_pass, :].bitcast(FP8X4),
-                    rhs_scale=act_scales[b][:, k_pass, :],
-                    start=(k_pass == passes[0]),
-                    stop=(k_pass == passes[-1]),
+        def copy_out_weights(g, passes):
+            grouped = w_stage.tile([P, len(passes), GROUP * UNIT * PACK], BF16, name="w_grouped%d" % len(passes), align_bytes=64)
+            w_grouped[(g, passes)] = grouped
+            for j, k_pass in enumerate(passes):
+                nc.scalar.copy(
+                    out=grouped[:, j, :].bitcast(F32).rearrange("p (i m u) -> p i m u", i=GROUP, u=2),
+                    in_=turned[(g, k_pass)][:].rearrange("p i u m -> p i m u"),
                 )
-            return acc
 
-        def multiply_main(b, c):
-            return multiply(b, c, (0,), "main")
-
-        def multiply_short(b, c):
-            return multiply(b, c, (1, 2), "short")
-
-        def norm_main(c, main):
-            main_bn = bn_stage.tile([P, POSITIONS], F32, name="main_bn")
-            nc.scalar.activation(
-                out=main_bn[:], in_=main[:], func=ACT.Identity, scale=gain[:, 0, c : c + 1], bias=shift[:, c : c + 1]
+        def quantise_weights(g, passes):
+            nc.vector.quantize_mx(
+                out=w_codes[:, g, passes[0] : passes[-1] + 1, :].rearrange("p k m -> p (k m)").bitcast(FP8X4),
+                scales=w_scales[:, g, passes[0] : passes[-1] + 1, :].rearrange("p k m -> p (k m)"),
+                in_=w_grouped[(g, passes)][:].rearrange("p k m -> p (k m)"),
             )
-            return main_bn
 
-        def add_short(c, short, main_bn, total):
+        def multiply(s, passes, name):
+            b, g = divmod(s, GROUPS)
+            products = []
+            for i in range(GROUP):
+                acc = banks.tile([P, POSITIONS], F32, name=name, tag="bank")
+                for k_pass in passes:
+                    nc.tensor.matmul_mx(
+                        out=acc[:],
+                        lhsT=w_codes[:, g, k_pass, i * UNIT : (i + 1) * UNIT].bitcast(FP8X4),
+                        lhsT_scale=w_scales[:, g, k_pass, i * UNIT : (i + 1) * UNIT],
+                        rhs=act_codes[b][:, k_pass, :].bitcast(FP8X4),
+                        rhs_scale=act_scales[b][:, k_pass, :],
+                        start=(k_pass == passes[0]),
+                        stop=(k_pass == passes[-1]),
+                    )
+                products.append(acc)
+            return products
+
+        mains = {}
+        main_bn = {}
+
+        def norm_main(s, i):
+            c = (s % GROUPS) * GROUP + i
+            normed = bn_stage.tile([P, POSITIONS], F32, name="normed")
+            main_bn[(s, i)] = normed
+            bias = 0.0 if s < LEAD else shift[:, c : c + 1]
+            nc.scalar.activation(out=normed[:], in_=mains[s][i][:], func=ACT.Identity, scale=gain[:, 0, c : c + 1], bias=bias)
+
+        def add_short(s, i, short, result):
+            c = (s % GROUPS) * GROUP + i
             nc.vector.scalar_tensor_tensor(
-                out=total, in0=short[:], scalar=gain[:, 1, c : c + 1], in1=main_bn[:], op0=ALU.mult, op1=ALU.add
+                out=result[:, i, :], in0=short[:], scalar=gain[:, 1, c : c + 1], in1=main_bn[(s, i)][:], op0=ALU.mult, op1=ALU.add
             )
 
-        def relu_and_store(b, slots, result, on_scalar):
-            if on_scalar:
-                nc.scalar.activation(out=result, in_=result, func=ACT.Relu)
+        def relu_and_store(s, result, i, n, engine):
+            part = result[:, i : i + n, :]
+            b, g = divmod(s, GROUPS)
+            if s < LEAD:
+                for j in range(n):
+                    c = g * GROUP + i + j
+                    nc.vector.tensor_scalar(
+                        out=part[:, j, :], in0=part[:, j, :], scalar1=shift[:, c : c + 1], scalar2=0.0, op0=ALU.add, op1=ALU.max
+                    )
+            elif engine == "scalar":
+                nc.scalar.activation(out=part, in_=part, func=ACT.Relu)
             else:
-                nc.vector.tensor_scalar_max(out=result, in0=result, scalar1=0.0)
-            nc.sync.dma_start(out=out_slots[b][:, slots, :], in_=result)
+                nc.vector.tensor_scalar_max(out=part, in0=part, scalar1=0.0)
+            nc.sync.dma_start(out=out_slots[b][:, g * GROUP + i : g * GROUP + i + n, :], in_=part)
+
+        MAIN, SHORT = (0,), (1, 2)
 
         spread = keep.tile([P, 2, SLOTS], F32)
         gain = keep.tile([P, 2, SLOTS], F32)
@@ -192,76 +220,73 @@ def tile_bottleneck_transformer_pb_kernel(
         shift = keep.tile([P, SLOTS], F32)
         nc.vector.tensor_scalar_add(out=spread[:], in0=vectors[:, V_VAR : V_VAR + 2, :], scalar1=EPS)
         nc.scalar.sqrt(out=spread[:], in_=spread[:])
-        transpose_weights(0, 0)
+        for g in range(LEAD):
+            transpose_weights(g, MAIN)
         regroup_activations(0, 0, WHOLE)
         nc.vector.reciprocal(out=gain[:], in_=spread[:])
-        copy_out_weights(0, 0)
+        for g in range(LEAD):
+            copy_out_weights(g, MAIN)
         quantise_activations(0, 0)
         nc.vector.tensor_mul(out=gain[:], in0=gain[:], in1=vectors[:, V_GAIN : V_GAIN + 2, :])
-        quantise_weights(0, 0)
-        mains = [multiply_main(0, c) for c in range(GROUP)]
-        nc.vector.tensor_mul(out=centre[:, 0, :], in0=gain[:, 0, :], in1=vectors[:, V_MEAN, :])
-        nc.vector.tensor_sub(out=centre[:, 1, :], in0=vectors[:, V_MEAN + 1, :], in1=vectors[:, V_BIAS, :])
+        quantise_weights(0, MAIN)
+        quantise_weights(1, MAIN)
+        quantise_weights(2, MAIN)
+        for s in range(LEAD):
+            mains[s] = multiply(s, MAIN, "main")
         regroup_activations(0, 1, SHARED)
-        nc.vector.tensor_mul(out=centre[:, 1, :], in0=centre[:, 1, :], in1=gain[:, 1, :])
-        nc.vector.tensor_add(out=shift[:], in0=vectors[:, V_SHIFT, :], in1=vectors[:, V_SHIFT + 1, :])
-        regroup_activations(0, 2, SHARED)
-        nc.vector.tensor_sub(out=shift[:], in0=shift[:], in1=centre[:, 0, :])
+        norm_main(0, 0)
+        norm_main(0, 1)
+        norm_main(1, 0)
+        transpose_weights(0, SHORT)
+        copy_out_weights(0, SHORT)
+        norm_main(1, 1)
+        transpose_weights(LEAD, MAIN)
+        transpose_weights(1, SHORT)
+        regroup_activations(0, 2, WHOLE)
         quantise_activations(0, 1)
-        nc.vector.tensor_sub(out=shift[:], in0=shift[:], in1=centre[:, 1, :])
-        for k_pass in (1, 2):
-            transpose_weights(0, k_pass)
-            copy_out_weights(0, k_pass)
         quantise_activations(0, 2)
-        quantise_weights(0, 1)
-        quantise_weights(0, 2)
-        for k_pass in range(PASSES):
-            transpose_weights(1, k_pass)
+        quantise_weights(0, SHORT)
+        nc.vector.tensor_sub(out=centre[:, 1, :], in0=vectors[:, V_MEAN + 1, :], in1=vectors[:, V_BIAS, :])
+        nc.vector.tensor_mul(out=centre[:, 0, :], in0=gain[:, 0, :], in1=vectors[:, V_MEAN, :])
+        nc.vector.tensor_add(out=shift[:], in0=vectors[:, V_SHIFT, :], in1=vectors[:, V_SHIFT + 1, :])
+        nc.vector.tensor_mul(out=centre[:, 1, :], in0=centre[:, 1, :], in1=gain[:, 1, :])
+        nc.vector.tensor_sub(out=shift[:], in0=shift[:], in1=centre[:, 0, :])
+        nc.vector.tensor_sub(out=shift[:], in0=shift[:], in1=centre[:, 1, :])
 
-        waiting = []
-        for g in range(GROUPS):
-            c0, c1 = g * GROUP, g * GROUP + 1
-            ahead = g + 1 < GROUPS
-            if ahead:
-                copy_out_weights(g + 1, 0)
-                quantise_weights(g + 1, 0)
-            if g > 0:
-                mains = [multiply_main(0, c) for c in (c0, c1)]
-            main_bn0 = norm_main(c0, mains[0])
-            if ahead:
-                copy_out_weights(g + 1, 1)
-                quantise_weights(g + 1, 1)
-            main_bn1 = norm_main(c1, mains[1])
-            if ahead:
-                copy_out_weights(g + 1, 2)
-            shorts = [multiply_short(0, c) for c in (c0, c1)]
+        RELUS = ("vector", "vector", "vector", "scalar", "vector", "scalar", "vector", "scalar", "scalar", "vector", "scalar", "vector", "scalar", "scalar", "scalar")
+        waiting = None
+        for s in range(STEPS):
+            ahead = s + LEAD
+            shorts = multiply(s, SHORT, "short")
+            if ahead - 1 < STEPS:
+                norm_main(ahead - 1, 0)
+            if ahead < GROUPS:
+                copy_out_weights(ahead, MAIN)
+                quantise_weights(ahead, MAIN)
+            if ahead - 1 < STEPS:
+                norm_main(ahead - 1, 1)
+            if ahead < STEPS:
+                mains[ahead] = multiply(ahead, MAIN, "main")
+            if s + 1 < GROUPS:
+                copy_out_weights(s + 1, SHORT)
+            if s + 2 == GROUPS:
+                quantise_weights(s + 1, SHORT)
             result = results.tile([P, GROUP, POSITIONS], F32, name="result")
-            add_short(c0, shorts[0], main_bn0, result[:, 0, :])
-            if ahead:
-                quantise_weights(g + 1, 2)
-            add_short(c1, shorts[1], main_bn1, result[:, 1, :])
-            if g + 2 < GROUPS:
-                for k_pass in range(PASSES):
-                    transpose_weights(g + 2, k_pass)
-            waiting.append((0, group_slots(g), result[:], g % 2 == 0))
-            if len(waiting) > 1:
-                relu_and_store(*waiting.pop(0))
-            if g >= 2 and g % 2 == 0:
-                quantise_activations(1, (g - 2) // 2)
-            if g < 2 * PASSES:
-                regroup_activations(1, g // 2, HALVES[g % 2])
-
-        for g in range(GROUPS):
-            c0, c1 = g * GROUP, g * GROUP + 1
-            mains = [multiply_main(1, c) for c in (c0, c1)]
-            main_bn0 = norm_main(c0, mains[0])
-            main_bn1 = norm_main(c1, mains[1])
-            shorts = [multiply_short(1, c) for c in (c0, c1)]
-            result = results.tile([P, GROUP, POSITIONS], F32, name="result")
-            add_short(c0, shorts[0], main_bn0, result[:, 0, :])
-            add_short(c1, shorts[1], main_bn1, result[:, 1, :])
-            relu_and_store(*waiting.pop(0))
-            if g + 1 < GROUPS:
-                waiting.append((1, group_slots(g), result[:], g % 2 == 0))
-        relu_and_store(1, slice(c0, c0 + 1), result[:, 0:1, :], True)
-        relu_and_store(1, slice(c1, c1 + 1), result[:, 1:2, :], False)
+            add_short(s, 0, shorts[0], result)
+            add_short(s, 1, shorts[1], result)
+            if s + 2 < GROUPS:
+                quantise_weights(s + 1, SHORT)
+            if ahead + 1 < GROUPS:
+                transpose_weights(ahead + 1, MAIN)
+            if s + 2 < GROUPS:
+                transpose_weights(s + 2, SHORT)
+            if s > 0:
+                relu_and_store(s - 1, waiting, 0, GROUP, RELUS[s - 1])
+            waiting = result
+            if s < GROUPS:
+                if s >= 2 and s % 2 == 0:
+                    quantise_activations(1, (s - 2) // 2)
+                if s < 2 * PASSES:
+                    regroup_activations(1, s // 2, HALVES[s % 2])
+        relu_and_store(STEPS - 1, result, 0, 1, "scalar")
+        relu_and_store(STEPS - 1, result, 1, 1, "vector")

@@ -82,18 +82,27 @@ def tile_bottleneck_transformer_pb_kernel(
 
         vectors = keep.tile([P, 9, SLOTS], BF16)
         V_VAR, V_GAIN, V_MEAN, V_SHIFT, V_BIAS = 0, 2, 4, 6, 8
-        for i, vec in enumerate((bn3_v, scbn_v, bn3_g, scbn_g, bn3_m, scbn_m, bn3_b, scbn_b, sc_b)):
-            queue = nc.scalar if i < V_MEAN else nc.gpsimd
-            queue.dma_start(out=vectors[:, i, :], in_=vec.rearrange("(p c) -> p c", c=SLOTS))
+        all_vectors = (bn3_v, scbn_v, bn3_g, scbn_g, bn3_m, scbn_m, bn3_b, scbn_b, sc_b)
+
+        def load_vector(queue, i):
+            queue.dma_start(out=vectors[:, i, :], in_=all_vectors[i].rearrange("(p c) -> p c", c=SLOTS))
+
+        for i in range(V_MEAN):
+            load_vector(nc.scalar, i)
 
         load_activations(0, 0)
         load_main_weights(0)
         load_main_weights(1)
         load_main_weights(2)
+        load_vector(nc.sync, V_MEAN)
         load_activations(0, 1)
+        load_vector(nc.sync, V_MEAN + 1)
         load_short_weights(0)
+        load_vector(nc.sync, V_SHIFT)
         load_activations(0, 2)
+        load_vector(nc.sync, V_SHIFT + 1)
         load_main_weights(3)
+        load_vector(nc.sync, V_BIAS)
         load_short_weights(1)
         load_main_weights(4)
         load_short_weights(2)
@@ -246,12 +255,6 @@ def tile_bottleneck_transformer_pb_kernel(
         quantise_activations(0, 1)
         quantise_activations(0, 2)
         quantise_weights(0, SHORT)
-        nc.vector.tensor_sub(out=centre[:, 1, :], in0=vectors[:, V_MEAN + 1, :], in1=vectors[:, V_BIAS, :])
-        nc.vector.tensor_mul(out=centre[:, 0, :], in0=gain[:, 0, :], in1=vectors[:, V_MEAN, :])
-        nc.vector.tensor_add(out=shift[:], in0=vectors[:, V_SHIFT, :], in1=vectors[:, V_SHIFT + 1, :])
-        nc.vector.tensor_mul(out=centre[:, 1, :], in0=centre[:, 1, :], in1=gain[:, 1, :])
-        nc.vector.tensor_sub(out=shift[:], in0=shift[:], in1=centre[:, 0, :])
-        nc.vector.tensor_sub(out=shift[:], in0=shift[:], in1=centre[:, 1, :])
 
         RELUS = ("vector", "vector", "vector", "scalar", "vector", "scalar", "vector", "scalar", "scalar", "vector", "scalar", "vector", "scalar", "scalar", "scalar")
         waiting = None
@@ -272,8 +275,17 @@ def tile_bottleneck_transformer_pb_kernel(
             if s + 2 == GROUPS:
                 quantise_weights(s + 1, SHORT)
             result = results.tile([P, GROUP, POSITIONS], F32, name="result")
+            if s == 0:
+                nc.vector.tensor_sub(out=centre[:, 1, :], in0=vectors[:, V_MEAN + 1, :], in1=vectors[:, V_BIAS, :])
+                nc.vector.tensor_mul(out=centre[:, 0, :], in0=gain[:, 0, :], in1=vectors[:, V_MEAN, :])
+                nc.vector.tensor_add(out=shift[:], in0=vectors[:, V_SHIFT, :], in1=vectors[:, V_SHIFT + 1, :])
             add_short(s, 0, shorts[0], result)
+            if s == 0:
+                nc.vector.tensor_mul(out=centre[:, 1, :], in0=centre[:, 1, :], in1=gain[:, 1, :])
+                nc.vector.tensor_sub(out=shift[:], in0=shift[:], in1=centre[:, 0, :])
             add_short(s, 1, shorts[1], result)
+            if s == 0:
+                nc.vector.tensor_sub(out=shift[:], in0=shift[:], in1=centre[:, 1, :])
             if s + 2 < GROUPS:
                 quantise_weights(s + 1, SHORT)
             if ahead + 1 < GROUPS:

@@ -26,6 +26,7 @@ GROUP = 2
 GROUPS = SLOTS // GROUP
 UNIT = P
 EPS = 1e-5
+F32_MAX = 3.4028234663852886e38
 STEPS = BATCH * GROUPS
 LEAD = 3
 
@@ -217,6 +218,8 @@ def tile_bottleneck_transformer_pb_kernel(
                     )
             elif engine == "scalar":
                 nc.scalar.activation(out=part, in_=part, func=ACT.Relu)
+            elif engine == "gpsimd":
+                nc.gpsimd.tensor_scalar(out=part, in0=part, scalar1=F32_MAX, scalar2=0.0, op0=ALU.min, op1=ALU.max)
             else:
                 nc.vector.tensor_scalar_max(out=part, in0=part, scalar1=0.0)
             nc.sync.dma_start(out=out_slots[b][:, g * GROUP + i : g * GROUP + i + n, :], in_=part)
@@ -256,7 +259,7 @@ def tile_bottleneck_transformer_pb_kernel(
         quantise_activations(0, 2)
         quantise_weights(0, SHORT)
 
-        RELUS = ("vector", "vector", "vector", "scalar", "vector", "scalar", "vector", "scalar", "scalar", "vector", "scalar", "vector", "scalar", "scalar", "scalar")
+        RELUS = ("vector", "vector", "vector", "scalar", "vector", "scalar", "vector", "scalar", "gpsimd", "gpsimd", "gpsimd", "gpsimd", "gpsimd", "gpsimd", "scalar")
         waiting = None
         for s in range(STEPS):
             ahead = s + LEAD

@@ -259,20 +259,26 @@ def tile_bottleneck_transformer_pb_kernel(
         quantise_activations(0, 2)
         quantise_weights(0, SHORT)
 
+        def lead(s):
+            return LEAD if s < GROUPS else max(1, LEAD - 1 - (s - GROUPS) // 2)
+
         RELUS = ("vector", "vector", "vector", "scalar", "vector", "scalar", "vector", "scalar", "gpsimd", "gpsimd", "gpsimd", "gpsimd", "gpsimd", "gpsimd", "scalar")
         waiting = None
+        TAIL = {14: ("gpsimd", "gpsimd"), 15: ("scalar", "vector")}
+        fresh = (LEAD - 1,)
         for s in range(STEPS):
             ahead = s + LEAD
             shorts = multiply(s, SHORT, "short")
-            if ahead - 1 < STEPS:
-                norm_main(ahead - 1, 0)
+            for m in fresh:
+                norm_main(m, 0)
             if ahead < GROUPS:
                 copy_out_weights(ahead, MAIN)
                 quantise_weights(ahead, MAIN)
-            if ahead - 1 < STEPS:
-                norm_main(ahead - 1, 1)
-            if ahead < STEPS:
-                mains[ahead] = multiply(ahead, MAIN, "main")
+            for m in fresh:
+                norm_main(m, 1)
+            fresh = range(len(mains), min(s + lead(s), STEPS - 1) + 1)
+            for m in fresh:
+                mains[m] = multiply(m, MAIN, "main")
             if s + 1 < GROUPS:
                 copy_out_weights(s + 1, SHORT)
             if s + 2 == GROUPS:
@@ -295,13 +301,14 @@ def tile_bottleneck_transformer_pb_kernel(
                 transpose_weights(ahead + 1, MAIN)
             if s + 2 < GROUPS:
                 transpose_weights(s + 2, SHORT)
-            if s > 0:
+            if 0 < s <= 14:
                 relu_and_store(s - 1, waiting, 0, GROUP, RELUS[s - 1])
             waiting = result
+            if s in TAIL:
+                for i in range(GROUP):
+                    relu_and_store(s, result, i, 1, TAIL[s][i])
             if s < GROUPS:
                 if s >= 2 and s % 2 == 0:
                     quantise_activations(1, (s - 2) // 2)
                 if s < 2 * PASSES:
                     regroup_activations(1, s // 2, HALVES[s % 2])
-        relu_and_store(STEPS - 1, result, 0, 1, "scalar")
-        relu_and_store(STEPS - 1, result, 1, 1, "vector")

@@ -88,23 +88,20 @@ def tile_bottleneck_transformer_pb_kernel(
         def load_vector(queue, i):
             queue.dma_start(out=vectors[:, i, :], in_=all_vectors[i].rearrange("(p c) -> p c", c=SLOTS))
 
-        for i in range(V_MEAN):
+        for i in range(V_VAR, V_MEAN):
             load_vector(nc.scalar, i)
 
         load_activations(0, 0)
         load_main_weights(0)
         load_main_weights(1)
         load_main_weights(2)
-        load_vector(nc.sync, V_MEAN)
         load_activations(0, 1)
-        load_vector(nc.sync, V_MEAN + 1)
         load_short_weights(0)
-        load_vector(nc.sync, V_SHIFT)
         load_activations(0, 2)
-        load_vector(nc.sync, V_SHIFT + 1)
         load_main_weights(3)
-        load_vector(nc.sync, V_BIAS)
         load_short_weights(1)
+        for i in range(V_MEAN, V_BIAS + 1):
+            load_vector(nc.sync, i)
         load_main_weights(4)
         load_short_weights(2)
         load_main_weights(5)
@@ -230,18 +227,19 @@ def tile_bottleneck_transformer_pb_kernel(
         gain = keep.tile([P, 2, SLOTS], F32)
         centre = keep.tile([P, 2, SLOTS], F32)
         shift = keep.tile([P, SLOTS], F32)
-        nc.vector.tensor_scalar_add(out=spread[:], in0=vectors[:, V_VAR : V_VAR + 2, :], scalar1=EPS)
-        nc.scalar.sqrt(out=spread[:], in_=spread[:])
         for g in range(LEAD):
             transpose_weights(g, MAIN)
         regroup_activations(0, 0, WHOLE)
-        nc.vector.reciprocal(out=gain[:], in_=spread[:])
-        for g in range(LEAD):
-            copy_out_weights(g, MAIN)
+        nc.vector.tensor_scalar_add(out=spread[:], in0=vectors[:, V_VAR : V_VAR + 2, :], scalar1=EPS)
+        copy_out_weights(0, MAIN)
+        nc.scalar.sqrt(out=spread[:], in_=spread[:])
+        copy_out_weights(1, MAIN)
+        copy_out_weights(2, MAIN)
         quantise_activations(0, 0)
-        nc.vector.tensor_mul(out=gain[:], in0=gain[:], in1=vectors[:, V_GAIN : V_GAIN + 2, :])
         quantise_weights(0, MAIN)
+        nc.vector.reciprocal(out=gain[:], in_=spread[:])
         quantise_weights(1, MAIN)
+        nc.vector.tensor_mul(out=gain[:], in0=gain[:], in1=vectors[:, V_GAIN : V_GAIN + 2, :])
         quantise_weights(2, MAIN)
         for s in range(LEAD):
             mains[s] = multiply(s, MAIN, "main")
@@ -254,13 +252,13 @@ def tile_bottleneck_transformer_pb_kernel(
         norm_main(1, 1)
         transpose_weights(LEAD, MAIN)
         transpose_weights(1, SHORT)
-        regroup_activations(0, 2, WHOLE)
         quantise_activations(0, 1)
-        quantise_activations(0, 2)
+        regroup_activations(0, 2, WHOLE)
         quantise_weights(0, SHORT)
+        quantise_activations(0, 2)
 
         def lead(s):
-            return LEAD if s < GROUPS else max(1, LEAD - 1 - (s - GROUPS) // 2)
+            return LEAD if s < GROUPS else max(1, LEAD - 1 - (s - GROUPS))
 
         RELUS = ("vector", "vector", "vector", "scalar", "vector", "scalar", "vector", "scalar", "gpsimd", "gpsimd", "gpsimd", "gpsimd", "gpsimd", "gpsimd", "scalar")
         waiting = None

@@ -41,7 +41,7 @@ def tile_bottleneck_transformer_pb_kernel(
         keep = ctx.enter_context(tc.tile_pool(name="keep", bufs=1))
         act_stage = ctx.enter_context(tc.tile_pool(name="act_stage", bufs=3))
         w_stage = ctx.enter_context(tc.tile_pool(name="w_stage", bufs=3))
-        bn_stage = ctx.enter_context(tc.tile_pool(name="bn_stage", bufs=2 * (LEAD + 2)))
+        bn_stage = ctx.enter_context(tc.tile_pool(name="bn_stage", bufs=2 * (LEAD + 3)))
         results = ctx.enter_context(tc.tile_pool(name="results", bufs=10))
         banks = ctx.enter_context(tc.psum_pool(name="banks", bufs=8))
         ctx.enter_context(tc.manual_schedule())
@@ -258,7 +258,7 @@ def tile_bottleneck_transformer_pb_kernel(
         quantise_activations(0, 2)
 
         def lead(s):
-            return LEAD if s < GROUPS else max(1, LEAD - 1 - (s - GROUPS))
+            return LEAD + (s >= GROUPS - 2) if s < GROUPS else max(1, LEAD - 1 - (s - GROUPS))
 
         RELUS = ("vector", "vector", "vector", "scalar", "vector", "scalar", "vector", "scalar", "gpsimd", "gpsimd", "gpsimd", "gpsimd", "gpsimd", "gpsimd", "scalar")
         waiting = None
@@ -272,6 +272,8 @@ def tile_bottleneck_transformer_pb_kernel(
             if ahead < GROUPS:
                 copy_out_weights(ahead, MAIN)
                 quantise_weights(ahead, MAIN)
+            if 1 <= s <= 2 * PASSES:
+                regroup_activations(1, (s - 1) // 2, HALVES[(s - 1) % 2])
             for m in fresh:
                 norm_main(m, 1)
             fresh = range(len(mains), min(s + lead(s), STEPS - 1) + 1)
@@ -308,5 +310,3 @@ def tile_bottleneck_transformer_pb_kernel(
             if s < GROUPS:
                 if s >= 2 and s % 2 == 0:
                     quantise_activations(1, (s - 2) // 2)
-                if s < 2 * PASSES:
-                    regroup_activations(1, s // 2, HALVES[s % 2])

@@ -24,11 +24,15 @@ C_OUT = 2048
 SLOTS = C_OUT // P
 GROUP = 2
 GROUPS = SLOTS // GROUP
-UNIT = P
+STEPS = BATCH * GROUPS
+MAIN, SHORT = (0,), (1, 2)
+LEAD = 3
+EARLY = LEAD + 1
+SPLIT_FROM = STEPS - 5
 EPS = 1e-5
 F32_MAX = 3.4028234663852886e38
-STEPS = BATCH * GROUPS
-LEAD = 3
+ALL = slice(0, POSITIONS)
+HALVES = (slice(0, POSITIONS // 2), slice(POSITIONS // 2, POSITIONS))
 
 FLOPS = 2 * BATCH * C_OUT * C_ALL * POSITIONS
 
@@ -53,8 +57,8 @@ def tile_bottleneck_transformer_pb_kernel(
         act_raw = [keep.tile([P, PASSES, PACK, POSITIONS], BF16, name="act_raw%d" % b) for b in range(BATCH)]
         act_codes = [keep.tile([P, PASSES, POSITIONS], U32, name="act_codes%d" % b, align_bytes=64) for b in range(BATCH)]
         act_scales = [keep.tile([P, PASSES, POSITIONS], U8, name="act_scales%d" % b, align_bytes=64) for b in range(BATCH)]
-        w_codes = keep.tile([P, GROUPS, PASSES, GROUP * UNIT], U32, align_bytes=64)
-        w_scales = keep.tile([P, GROUPS, PASSES, GROUP * UNIT], U8, align_bytes=64)
+        w_codes = keep.tile([P, GROUPS, PASSES, GROUP * P], U32, align_bytes=64)
+        w_scales = keep.tile([P, GROUPS, PASSES, GROUP * P], U8, align_bytes=64)
         out_slots = [out[b].rearrange("(p c) n -> p c n", c=SLOTS) for b in range(BATCH)]
 
         def group_slots(g):
@@ -65,10 +69,6 @@ def tile_bottleneck_transformer_pb_kernel(
 
         def load_short_weights(g):
             nc.sync.dma_start(out=short_raw[g][:], in_=sc_slots[:, group_slots(g), :])
-
-        def load_weights(g):
-            load_main_weights(g)
-            load_short_weights(g)
 
         def load_activations(b, k_pass):
             rows = h_attn[b] if k_pass == 0 else x[b, (k_pass - 1) * K_PASS : k_pass * K_PASS, :]
@@ -118,20 +118,13 @@ def tile_bottleneck_transformer_pb_kernel(
 
         act_grouped = {}
 
-        def regroup_activations(b, k_pass, shares):
-            grouped = act_grouped.get((b, k_pass))
-            if grouped is None:
-                grouped = act_stage.tile([P, POSITIONS, PACK], BF16, name="act_grouped", align_bytes=64)
-                act_grouped[(b, k_pass)] = grouped
-            for copy, first, end in shares:
-                copy(
-                    out=grouped[:, first:end, :].rearrange("p (c i) t -> p c t i", i=4),
-                    in_=act_raw[b][:, k_pass, :, first:end].rearrange("p t (c i) -> p c t i", i=4),
-                )
-
-        WHOLE = ((nc.vector.tensor_copy, 0, POSITIONS),)
-        SHARED = ((nc.vector.tensor_copy, 0, 352), (nc.scalar.copy, 352, POSITIONS))
-        HALVES = (((nc.vector.tensor_copy, 0, 256),), ((nc.vector.tensor_copy, 256, POSITIONS),))
+        def regroup_activations(b, k_pass, cols=ALL):
+            if (b, k_pass) not in act_grouped:
+                act_grouped[(b, k_pass)] = act_stage.tile([P, POSITIONS, PACK], BF16, name="act_grouped", align_bytes=64)
+            nc.vector.tensor_copy(
+                out=act_grouped[(b, k_pass)][:, cols, :].rearrange("p (c i) t -> p c t i", i=4),
+                in_=act_raw[b][:, k_pass, :, cols].rearrange("p t (c i) -> p c t i", i=4),
+            )
 
         def quantise_activations(b, k_pass):
             nc.vector.quantize_mx(
@@ -155,7 +148,7 @@ def tile_bottleneck_transformer_pb_kernel(
         w_grouped = {}
 
         def copy_out_weights(g, passes):
-            grouped = w_stage.tile([P, len(passes), GROUP * UNIT * PACK], BF16, name="w_grouped%d" % len(passes), align_bytes=64)
+            grouped = w_stage.tile([P, len(passes), GROUP * P * PACK], BF16, name="w_grouped%d" % len(passes), align_bytes=64)
             w_grouped[(g, passes)] = grouped
             for j, k_pass in enumerate(passes):
                 nc.scalar.copy(
@@ -178,8 +171,8 @@ def tile_bottleneck_transformer_pb_kernel(
                 for k_pass in passes:
                     nc.tensor.matmul_mx(
                         out=acc[:],
-                        lhsT=w_codes[:, g, k_pass, i * UNIT : (i + 1) * UNIT].bitcast(FP8X4),
-                        lhsT_scale=w_scales[:, g, k_pass, i * UNIT : (i + 1) * UNIT],
+                        lhsT=w_codes[:, g, k_pass, i * P : (i + 1) * P].bitcast(FP8X4),
+                        lhsT_scale=w_scales[:, g, k_pass, i * P : (i + 1) * P],
                         rhs=act_codes[b][:, k_pass, :].bitcast(FP8X4),
                         rhs_scale=act_scales[b][:, k_pass, :],
                         start=(k_pass == passes[0]),
@@ -195,33 +188,39 @@ def tile_bottleneck_transformer_pb_kernel(
             c = (s % GROUPS) * GROUP + i
             normed = bn_stage.tile([P, POSITIONS], F32, name="normed")
             main_bn[(s, i)] = normed
-            bias = 0.0 if s < LEAD else shift[:, c : c + 1]
+            bias = 0.0 if s < EARLY else shift[:, c : c + 1]
             nc.scalar.activation(out=normed[:], in_=mains[s][i][:], func=ACT.Identity, scale=gain[:, 0, c : c + 1], bias=bias)
 
-        def add_short(s, i, short, result):
+        def add_short(s, i, short, result, cols=ALL):
             c = (s % GROUPS) * GROUP + i
             nc.vector.scalar_tensor_tensor(
-                out=result[:, i, :], in0=short[:], scalar=gain[:, 1, c : c + 1], in1=main_bn[(s, i)][:], op0=ALU.mult, op1=ALU.add
+                out=result[:, i, cols],
+                in0=short[:, cols],
+                scalar=gain[:, 1, c : c + 1],
+                in1=main_bn[(s, i)][:, cols],
+                op0=ALU.mult,
+                op1=ALU.add,
             )
 
-        def relu_and_store(s, result, i, n, engine):
-            part = result[:, i : i + n, :]
+        def relu_and_store(s, result, i, n, engine, cols=ALL):
+            part = result[:, i : i + n, cols]
             b, g = divmod(s, GROUPS)
-            if s < LEAD:
+            if s < EARLY:
                 for j in range(n):
-                    c = g * GROUP + i + j
-                    nc.vector.tensor_scalar(
-                        out=part[:, j, :], in0=part[:, j, :], scalar1=shift[:, c : c + 1], scalar2=0.0, op0=ALU.add, op1=ALU.max
-                    )
+                    bias = shift[:, g * GROUP + i + j : g * GROUP + i + j + 1]
+                    if engine == "scalar":
+                        nc.scalar.activation(out=part[:, j, :], in_=part[:, j, :], func=ACT.Relu, bias=bias)
+                    else:
+                        nc.vector.tensor_scalar(
+                            out=part[:, j, :], in0=part[:, j, :], scalar1=bias, scalar2=0.0, op0=ALU.add, op1=ALU.max
+                        )
             elif engine == "scalar":
                 nc.scalar.activation(out=part, in_=part, func=ACT.Relu)
             elif engine == "gpsimd":
                 nc.gpsimd.tensor_scalar(out=part, in0=part, scalar1=F32_MAX, scalar2=0.0, op0=ALU.min, op1=ALU.max)
             else:
                 nc.vector.tensor_scalar_max(out=part, in0=part, scalar1=0.0)
-            nc.sync.dma_start(out=out_slots[b][:, g * GROUP + i : g * GROUP + i + n, :], in_=part)
-
-        MAIN, SHORT = (0,), (1, 2)
+            nc.sync.dma_start(out=out_slots[b][:, g * GROUP + i : g * GROUP + i + n, cols], in_=part)
 
         spread = keep.tile([P, 2, SLOTS], F32)
         gain = keep.tile([P, 2, SLOTS], F32)
@@ -229,7 +228,7 @@ def tile_bottleneck_transformer_pb_kernel(
         shift = keep.tile([P, SLOTS], F32)
         for g in range(LEAD):
             transpose_weights(g, MAIN)
-        regroup_activations(0, 0, WHOLE)
+        regroup_activations(0, 0)
         nc.vector.tensor_scalar_add(out=spread[:], in0=vectors[:, V_VAR : V_VAR + 2, :], scalar1=EPS)
         copy_out_weights(0, MAIN)
         nc.scalar.sqrt(out=spread[:], in_=spread[:])
@@ -243,7 +242,7 @@ def tile_bottleneck_transformer_pb_kernel(
         quantise_weights(2, MAIN)
         for s in range(LEAD):
             mains[s] = multiply(s, MAIN, "main")
-        regroup_activations(0, 1, SHARED)
+        regroup_activations(0, 1)
         norm_main(0, 0)
         norm_main(0, 1)
         norm_main(1, 0)
@@ -253,16 +252,17 @@ def tile_bottleneck_transformer_pb_kernel(
         transpose_weights(LEAD, MAIN)
         transpose_weights(1, SHORT)
         quantise_activations(0, 1)
-        regroup_activations(0, 2, WHOLE)
+        regroup_activations(0, 2)
         quantise_weights(0, SHORT)
         quantise_activations(0, 2)
+
+        def relu_engine(s):
+            return "gpsimd" if s >= GROUPS else "scalar" if s % 2 else "vector"
 
         def lead(s):
             return LEAD + (s >= GROUPS - 2) if s < GROUPS else max(1, LEAD - 1 - (s - GROUPS))
 
-        RELUS = ("vector", "vector", "vector", "scalar", "vector", "scalar", "vector", "scalar", "gpsimd", "gpsimd", "gpsimd", "gpsimd", "gpsimd", "gpsimd", "scalar")
         waiting = None
-        TAIL = {14: ("gpsimd", "gpsimd"), 15: ("scalar", "vector")}
         fresh = (LEAD - 1,)
         for s in range(STEPS):
             ahead = s + LEAD
@@ -276,6 +276,8 @@ def tile_bottleneck_transformer_pb_kernel(
                 regroup_activations(1, (s - 1) // 2, HALVES[(s - 1) % 2])
             for m in fresh:
                 norm_main(m, 1)
+            if s > SPLIT_FROM:
+                relu_and_store(s - 1, waiting, 1, 1, "scalar")
             fresh = range(len(mains), min(s + lead(s), STEPS - 1) + 1)
             for m in fresh:
                 mains[m] = multiply(m, MAIN, "main")
@@ -292,7 +294,8 @@ def tile_bottleneck_transformer_pb_kernel(
             if s == 0:
                 nc.vector.tensor_mul(out=centre[:, 1, :], in0=centre[:, 1, :], in1=gain[:, 1, :])
                 nc.vector.tensor_sub(out=shift[:], in0=shift[:], in1=centre[:, 0, :])
-            add_short(s, 1, shorts[1], result)
+            for cols in HALVES if s == STEPS - 1 else (ALL,):
+                add_short(s, 1, shorts[1], result, cols)
             if s == 0:
                 nc.vector.tensor_sub(out=shift[:], in0=shift[:], in1=centre[:, 1, :])
             if s + 2 < GROUPS:
@@ -301,12 +304,14 @@ def tile_bottleneck_transformer_pb_kernel(
                 transpose_weights(ahead + 1, MAIN)
             if s + 2 < GROUPS:
                 transpose_weights(s + 2, SHORT)
-            if 0 < s <= 14:
-                relu_and_store(s - 1, waiting, 0, GROUP, RELUS[s - 1])
+            if 0 < s <= SPLIT_FROM:
+                relu_and_store(s - 1, waiting, 0, GROUP, relu_engine(s - 1))
             waiting = result
-            if s in TAIL:
-                for i in range(GROUP):
-                    relu_and_store(s, result, i, 1, TAIL[s][i])
+            if SPLIT_FROM <= s < STEPS - 1:
+                relu_and_store(s, result, 0, 1, "gpsimd")
             if s < GROUPS:
                 if s >= 2 and s % 2 == 0:
                     quantise_activations(1, (s - 2) // 2)
+        relu_and_store(STEPS - 1, result, 0, 1, "scalar")
+        for cols in HALVES:
+            relu_and_store(STEPS - 1, result, 1, 1, "vector", cols)

@@ -133,6 +133,14 @@ def tile_bottleneck_transformer_pb_kernel(
                 in_=act_grouped[(b, k_pass)][:].rearrange("p n t -> p (n t)"),
             )
 
+        zeros = keep.tile([P, POSITIONS], BF16)
+        nc.vector.memset(zeros[:], 0.0)
+
+        def keep_warm(n):
+            unread = banks.tile([P, POSITIONS], F32, name="unread", tag="bank")
+            for i in range(n):
+                nc.tensor.matmul(out=unread[:], lhsT=zeros[:, 0:P], rhs=zeros[:], start=True, stop=True)
+
         turned = {}
 
         def transpose_weights(g, passes):
@@ -226,8 +234,10 @@ def tile_bottleneck_transformer_pb_kernel(
         gain = keep.tile([P, 2, SLOTS], F32)
         centre = keep.tile([P, 2, SLOTS], F32)
         shift = keep.tile([P, SLOTS], F32)
+        keep_warm(8)
         for g in range(LEAD):
             transpose_weights(g, MAIN)
+        keep_warm(3)
         regroup_activations(0, 0)
         nc.vector.tensor_scalar_add(out=spread[:], in0=vectors[:, V_VAR : V_VAR + 2, :], scalar1=EPS)
         copy_out_weights(0, MAIN)
@@ -250,7 +260,9 @@ def tile_bottleneck_transformer_pb_kernel(
         copy_out_weights(0, SHORT)
         norm_main(1, 1)
         transpose_weights(LEAD, MAIN)
+        keep_warm(1)
         transpose_weights(1, SHORT)
+        keep_warm(1)
         quantise_activations(0, 1)
         regroup_activations(0, 2)
         quantise_weights(0, SHORT)

from contextlib import ExitStack

import concourse.mybir as mybir
from concourse.masks import make_identity

F32 = mybir.dt.float32
BF16 = mybir.dt.bfloat16
U32 = mybir.dt.uint32
U8 = mybir.dt.uint8
FP8X4 = mybir.dt.float8_e4m3fn_x4
ACT = mybir.ActivationFunctionType
ALU = mybir.AluOpType

P = 128
PACK = 4
K_PASS = P * PACK
BATCH = 2
POSITIONS = 512
C_MAIN = 512
C_SHORT = 1024
C_ALL = C_MAIN + C_SHORT
PASSES = C_ALL // K_PASS
C_OUT = 2048
SLOTS = C_OUT // P
GROUP = 2
GROUPS = SLOTS // GROUP
STEPS = BATCH * GROUPS
MAIN, SHORT = (0,), (1, 2)
LEAD = 3
EARLY = LEAD + 1
SPLIT_FROM = STEPS - 5
EPS = 1e-5
F32_MAX = 3.4028234663852886e38
ALL = slice(0, POSITIONS)
HALVES = (slice(0, POSITIONS // 2), slice(POSITIONS // 2, POSITIONS))

FLOPS = 2 * BATCH * C_OUT * C_ALL * POSITIONS


def tile_bottleneck_transformer_pb_kernel(
    tc, h_attn, x, conv3_w, bn3_g, bn3_b, bn3_m, bn3_v, sc_w, sc_b, scbn_g, scbn_b, scbn_m, scbn_v, out
):
    nc = tc.nc
    with ExitStack() as ctx:
        keep = ctx.enter_context(tc.tile_pool(name="keep", bufs=1))
        act_stage = ctx.enter_context(tc.tile_pool(name="act_stage", bufs=3))
        w_stage = ctx.enter_context(tc.tile_pool(name="w_stage", bufs=3))
        bn_stage = ctx.enter_context(tc.tile_pool(name="bn_stage", bufs=2 * (LEAD + 3)))
        results = ctx.enter_context(tc.tile_pool(name="results", bufs=10))
        banks = ctx.enter_context(tc.psum_pool(name="banks", bufs=8))
        ctx.enter_context(tc.manual_schedule())

        main_raw = [keep.tile([P, GROUP, C_MAIN], BF16, name="main_raw%d" % g) for g in range(GROUPS)]
        short_raw = [keep.tile([P, GROUP, C_SHORT], BF16, name="short_raw%d" % g) for g in range(GROUPS)]
        conv3_slots = conv3_w.rearrange("(p c) k -> p c k", c=SLOTS)
        sc_slots = sc_w.rearrange("(p c) k -> p c k", c=SLOTS)
        act_raw = [keep.tile([P, PASSES, PACK, POSITIONS], BF16, name="act_raw%d" % b) for b in range(BATCH)]
        act_codes = [keep.tile([P, PASSES, POSITIONS], U32, name="act_codes%d" % b, align_bytes=64) for b in range(BATCH)]
        act_scales = [keep.tile([P, PASSES, POSITIONS], U8, name="act_scales%d" % b, align_bytes=64) for b in range(BATCH)]
        w_codes = keep.tile([P, GROUPS, PASSES, GROUP * P], U32, align_bytes=64)
        w_scales = keep.tile([P, GROUPS, PASSES, GROUP * P], U8, align_bytes=64)
        out_slots = [out[b].rearrange("(p c) n -> p c n", c=SLOTS) for b in range(BATCH)]

        def group_slots(g):
            return slice(g * GROUP, (g + 1) * GROUP)

        def load_main_weights(g):
            nc.sync.dma_start(out=main_raw[g][:], in_=conv3_slots[:, group_slots(g), :])

        def load_short_weights(g):
            nc.sync.dma_start(out=short_raw[g][:], in_=sc_slots[:, group_slots(g), :])

        def load_activations(b, k_pass):
            rows = h_attn[b] if k_pass == 0 else x[b, (k_pass - 1) * K_PASS : k_pass * K_PASS, :]
            nc.sync.dma_start(out=act_raw[b][:, k_pass], in_=rows.rearrange("(p t) n -> p t n", t=PACK))

        dummy = keep.tile([P, 2], F32)
        nc.vector.memset(dummy[:, 0:1], 1.0)
        nc.scalar.sqrt(out=dummy[:, 1:2], in_=dummy[:, 0:1])

        identity = keep.tile([P, P], F32)
        make_identity(nc, identity[:])

        vectors = keep.tile([P, 9, SLOTS], BF16)
        V_VAR, V_GAIN, V_MEAN, V_SHIFT, V_BIAS = 0, 2, 4, 6, 8
        all_vectors = (bn3_v, scbn_v, bn3_g, scbn_g, bn3_m, scbn_m, bn3_b, scbn_b, sc_b)

        def load_vector(queue, i):
            queue.dma_start(out=vectors[:, i, :], in_=all_vectors[i].rearrange("(p c) -> p c", c=SLOTS))

        for i in range(V_VAR, V_MEAN):
            load_vector(nc.scalar, i)

        load_activations(0, 0)
        load_main_weights(0)
        load_main_weights(1)
        load_main_weights(2)
        load_activations(0, 1)
        load_short_weights(0)
        load_activations(0, 2)
        load_main_weights(3)
        load_short_weights(1)
        for i in range(V_MEAN, V_BIAS + 1):
            load_vector(nc.sync, i)
        load_main_weights(4)
        load_short_weights(2)
        load_main_weights(5)
        load_activations(1, 0)
        load_short_weights(3)
        load_main_weights(6)
        load_activations(1, 1)
        load_short_weights(4)
        load_main_weights(7)
        load_short_weights(5)
        load_activations(1, 2)
        load_short_weights(6)
        load_short_weights(7)

        act_grouped = {}

        def regroup_activations(b, k_pass, cols=ALL):
            if (b, k_pass) not in act_grouped:
                act_grouped[(b, k_pass)] = act_stage.tile([P, POSITIONS, PACK], BF16, name="act_grouped", align_bytes=64)
            nc.vector.tensor_copy(
                out=act_grouped[(b, k_pass)][:, cols, :].rearrange("p (c i) t -> p c t i", i=4),
                in_=act_raw[b][:, k_pass, :, cols].rearrange("p t (c i) -> p c t i", i=4),
            )

        def quantise_activations(b, k_pass):
            nc.vector.quantize_mx(
                out=act_codes[b][:, k_pass, :].bitcast(FP8X4),
                scales=act_scales[b][:, k_pass, :],
                in_=act_grouped[(b, k_pass)][:].rearrange("p n t -> p (n t)"),
            )

        zeros = keep.tile([P, POSITIONS], BF16)
        nc.vector.memset(zeros[:], 0.0)

        def keep_warm(n):
            unread = banks.tile([P, POSITIONS], F32, name="unread", tag="bank")
            for i in range(n):
                nc.tensor.matmul(out=unread[:], lhsT=zeros[:, 0:P], rhs=zeros[:], start=True, stop=True)

        turned = {}

        def transpose_weights(g, passes):
            for k_pass in passes:
                bank = banks.tile([P, GROUP, 2, P], F32, name="turned", tag="bank")
                turned[(g, k_pass)] = bank
                raw, first = (main_raw[g], 0) if k_pass == 0 else (short_raw[g], (k_pass - 1) * K_PASS)
                for i in range(GROUP):
                    words = raw[:, i, first : first + K_PASS].bitcast(F32)
                    for u in range(2):
                        nc.tensor.transpose(bank[:, i, u, :], words[:, u : 2 * P : 2], identity[:])

        w_grouped = {}

        def copy_out_weights(g, passes):
            grouped = w_stage.tile([P, len(passes), GROUP * P * PACK], BF16, name="w_grouped%d" % len(passes), align_bytes=64)
            w_grouped[(g, passes)] = grouped
            for j, k_pass in enumerate(passes):
                nc.scalar.copy(
                    out=grouped[:, j, :].bitcast(F32).rearrange("p (i m u) -> p i m u", i=GROUP, u=2),
                    in_=turned[(g, k_pass)][:].rearrange("p i u m -> p i m u"),
                )

        def quantise_weights(g, passes):
            nc.vector.quantize_mx(
                out=w_codes[:, g, passes[0] : passes[-1] + 1, :].rearrange("p k m -> p (k m)").bitcast(FP8X4),
                scales=w_scales[:, g, passes[0] : passes[-1] + 1, :].rearrange("p k m -> p (k m)"),
                in_=w_grouped[(g, passes)][:].rearrange("p k m -> p (k m)"),
            )

        def multiply(s, passes, name):
            b, g = divmod(s, GROUPS)
            products = []
            for i in range(GROUP):
                acc = banks.tile([P, POSITIONS], F32, name=name, tag="bank")
                for k_pass in passes:
                    nc.tensor.matmul_mx(
                        out=acc[:],
                        lhsT=w_codes[:, g, k_pass, i * P : (i + 1) * P].bitcast(FP8X4),
                        lhsT_scale=w_scales[:, g, k_pass, i * P : (i + 1) * P],
                        rhs=act_codes[b][:, k_pass, :].bitcast(FP8X4),
                        rhs_scale=act_scales[b][:, k_pass, :],
                        start=(k_pass == passes[0]),
                        stop=(k_pass == passes[-1]),
                    )
                products.append(acc)
            return products

        mains = {}
        main_bn = {}

        def norm_main(s, i):
            c = (s % GROUPS) * GROUP + i
            normed = bn_stage.tile([P, POSITIONS], F32, name="normed")
            main_bn[(s, i)] = normed
            bias = 0.0 if s < EARLY else shift[:, c : c + 1]
            nc.scalar.activation(out=normed[:], in_=mains[s][i][:], func=ACT.Identity, scale=gain[:, 0, c : c + 1], bias=bias)

        def add_short(s, i, short, result, cols=ALL):
            c = (s % GROUPS) * GROUP + i
            nc.vector.scalar_tensor_tensor(
                out=result[:, i, cols],
                in0=short[:, cols],
                scalar=gain[:, 1, c : c + 1],
                in1=main_bn[(s, i)][:, cols],
                op0=ALU.mult,
                op1=ALU.add,
            )

        def relu_and_store(s, result, i, n, engine, cols=ALL):
            part = result[:, i : i + n, cols]
            b, g = divmod(s, GROUPS)
            if s < EARLY:
                for j in range(n):
                    bias = shift[:, g * GROUP + i + j : g * GROUP + i + j + 1]
                    if engine == "scalar":
                        nc.scalar.activation(out=part[:, j, :], in_=part[:, j, :], func=ACT.Relu, bias=bias)
                    else:
                        nc.vector.tensor_scalar(
                            out=part[:, j, :], in0=part[:, j, :], scalar1=bias, scalar2=0.0, op0=ALU.add, op1=ALU.max
                        )
            elif engine == "scalar":
                nc.scalar.activation(out=part, in_=part, func=ACT.Relu)
            elif engine == "gpsimd":
                nc.gpsimd.tensor_scalar(out=part, in0=part, scalar1=F32_MAX, scalar2=0.0, op0=ALU.min, op1=ALU.max)
            else:
                nc.vector.tensor_scalar_max(out=part, in0=part, scalar1=0.0)
            nc.sync.dma_start(out=out_slots[b][:, g * GROUP + i : g * GROUP + i + n, cols], in_=part)

        spread = keep.tile([P, 2, SLOTS], F32)
        gain = keep.tile([P, 2, SLOTS], F32)
        centre = keep.tile([P, 2, SLOTS], F32)
        shift = keep.tile([P, SLOTS], F32)
        keep_warm(8)
        for g in range(LEAD):
            transpose_weights(g, MAIN)
        keep_warm(3)
        regroup_activations(0, 0)
        nc.vector.tensor_scalar_add(out=spread[:], in0=vectors[:, V_VAR : V_VAR + 2, :], scalar1=EPS)
        copy_out_weights(0, MAIN)
        nc.scalar.sqrt(out=spread[:], in_=spread[:])
        copy_out_weights(1, MAIN)
        copy_out_weights(2, MAIN)
        quantise_activations(0, 0)
        quantise_weights(0, MAIN)
        nc.vector.reciprocal(out=gain[:], in_=spread[:])
        quantise_weights(1, MAIN)
        nc.vector.tensor_mul(out=gain[:], in0=gain[:], in1=vectors[:, V_GAIN : V_GAIN + 2, :])
        quantise_weights(2, MAIN)
        for s in range(LEAD):
            mains[s] = multiply(s, MAIN, "main")
        regroup_activations(0, 1)
        norm_main(0, 0)
        norm_main(0, 1)
        norm_main(1, 0)
        transpose_weights(0, SHORT)
        copy_out_weights(0, SHORT)
        norm_main(1, 1)
        transpose_weights(LEAD, MAIN)
        keep_warm(1)
        transpose_weights(1, SHORT)
        keep_warm(1)
        quantise_activations(0, 1)
        regroup_activations(0, 2)
        quantise_weights(0, SHORT)
        quantise_activations(0, 2)

        def relu_engine(s):
            return "gpsimd" if s >= GROUPS else "scalar" if s % 2 else "vector"

        def lead(s):
            return LEAD + (s >= GROUPS - 2) if s < GROUPS else max(1, LEAD - 1 - (s - GROUPS))

        waiting = None
        fresh = (LEAD - 1,)
        for s in range(STEPS):
            ahead = s + LEAD
            shorts = multiply(s, SHORT, "short")
            for m in fresh:
                norm_main(m, 0)
            if ahead < GROUPS:
                copy_out_weights(ahead, MAIN)
                quantise_weights(ahead, MAIN)
            if 1 <= s <= 2 * PASSES:
                regroup_activations(1, (s - 1) // 2, HALVES[(s - 1) % 2])
            for m in fresh:
                norm_main(m, 1)
            if s > SPLIT_FROM:
                relu_and_store(s - 1, waiting, 1, 1, "scalar")
            fresh = range(len(mains), min(s + lead(s), STEPS - 1) + 1)
            for m in fresh:
                mains[m] = multiply(m, MAIN, "main")
            if s + 1 < GROUPS:
                copy_out_weights(s + 1, SHORT)
            if s + 2 == GROUPS:
                quantise_weights(s + 1, SHORT)
            result = results.tile([P, GROUP, POSITIONS], F32, name="result")
            if s == 0:
                nc.vector.tensor_sub(out=centre[:, 1, :], in0=vectors[:, V_MEAN + 1, :], in1=vectors[:, V_BIAS, :])
                nc.vector.tensor_mul(out=centre[:, 0, :], in0=gain[:, 0, :], in1=vectors[:, V_MEAN, :])
                nc.vector.tensor_add(out=shift[:], in0=vectors[:, V_SHIFT, :], in1=vectors[:, V_SHIFT + 1, :])
            add_short(s, 0, shorts[0], result)
            if s == 0:
                nc.vector.tensor_mul(out=centre[:, 1, :], in0=centre[:, 1, :], in1=gain[:, 1, :])
                nc.vector.tensor_sub(out=shift[:], in0=shift[:], in1=centre[:, 0, :])
            for cols in HALVES if s == STEPS - 1 else (ALL,):
                add_short(s, 1, shorts[1], result, cols)
            if s == 0:
                nc.vector.tensor_sub(out=shift[:], in0=shift[:], in1=centre[:, 1, :])
            if s + 2 < GROUPS:
                quantise_weights(s + 1, SHORT)
            if ahead + 1 < GROUPS:
                transpose_weights(ahead + 1, MAIN)
            if s + 2 < GROUPS:
                transpose_weights(s + 2, SHORT)
            if 0 < s <= SPLIT_FROM:
                relu_and_store(s - 1, waiting, 0, GROUP, relu_engine(s - 1))
            waiting = result
            if SPLIT_FROM <= s < STEPS - 1:
                relu_and_store(s, result, 0, 1, "gpsimd")
            if s < GROUPS:
                if s >= 2 and s % 2 == 0:
                    quantise_activations(1, (s - 2) // 2)
        relu_and_store(STEPS - 1, result, 0, 1, "scalar")
        for cols in HALVES:
            relu_and_store(STEPS - 1, result, 1, 1, "vector", cols)
